import numpy as np
import ml_dtypes

BF16 = ml_dtypes.bfloat16


def bf(x):
    return np.asarray(x, np.float32).astype(BF16)


def f32(x):
    return np.asarray(x, np.float32)


def f64(x):
    return np.asarray(x).astype(np.float64)


def striped(idx):
    return np.tile(idx.reshape(-1, 16).T, (8, 1))


E, R, K, V, N = 128, 7, 3, 512, 1024


def setup_inputs():
    return {"u": f32(np.random.standard_normal((R * E, V))), "seq_emb": f32(np.random.standard_normal((E, N))), "offs": striped(np.random.permutation(np.tile(np.arange(V), 2))[:N])}


def reference(u, seq_emb, offs):
    idx = offs[:16].T.reshape(-1)
    rad = R // 2
    padded = np.pad(f64(seq_emb), ((0, 0), (rad, rad)))
    ctx = f64(u).reshape(R, E, V)[:, :, idx]
    proj = np.stack([padded[:, i:i + N] for i in range(R)], axis=0) * ctx
    return np.concatenate([proj[m:R - m].max(axis=0) for m in range(K)], axis=0)

@@ -1,0 +1,119 @@
+import concourse.mybir as mybir
+from concourse.masks import make_identity
+
+FEATURES = 128
+PLACES = 7
+MIDDLE = PLACES // 2
+WORDS = 512
+TOKENS = 1024
+PIECE = 512
+PER_COLUMN = 16
+MARGIN = 8
+SHARE = 384
+OUTER_RINGS = (1, 0)
+
+F32 = mybir.dt.float32
+U16 = mybir.dt.uint16
+MULT = mybir.AluOpType.mult
+MAX = mybir.AluOpType.max
+RELU = mybir.ActivationFunctionType.Relu
+
+
+def tile_multiregionembeddinglayer_kernel(tc, u, seq_emb, offs, out):
+    nc = tc.nc
+    pieces = range(0, TOKENS, PIECE)
+    inner = [MIDDLE - 1, MIDDLE, MIDDLE + 1]
+    outer = [place for ring in OUTER_RINGS for place in (ring, PLACES - 1 - ring)]
+    with (
+        tc.tile_pool(name="held", bufs=1) as held,
+        tc.tile_pool(name="products", bufs=2) as products,
+        tc.tile_pool(name="maxima", bufs=2) as maxima,
+        tc.psum_pool(name="differences", bufs=2) as differences,
+        tc.psum_pool(name="pairs", bufs=2) as pairs,
+    ):
+        offsets = held.tile([FEATURES, TOKENS // PER_COLUMN], U16, name="offsets")
+        sequence = held.tile([FEATURES, MARGIN + TOKENS + MARGIN], F32, name="sequence")
+        units = {place: held.tile([FEATURES, WORDS], F32, name=f"unit{place}") for place in outer + inner}
+        plus = held.tile([FEATURES, FEATURES], F32, name="plus")
+        minus = held.tile([FEATURES, FEATURES], F32, name="minus")
+
+        def tokens(start, stop):
+            return sequence[:, MARGIN + start : MARGIN + stop], seq_emb[:, start:stop]
+
+        def unit(place):
+            return units[place][:], u[place * FEATURES : (place + 1) * FEATURES, :]
+
+        nc.sync.dma_start(offsets[:], offs)
+        loads = [tokens(0, PIECE + MARGIN), unit(outer[0]), unit(outer[1]), tokens(PIECE + MARGIN, TOKENS)]
+        loads += [unit(place) for place in outer[2:] + inner]
+        for turn, (tile_side, dram_side) in enumerate(loads):
+            queue = nc.scalar if turn % 2 == 0 else nc.sync
+            queue.dma_start(tile_side, dram_side)
+        nc.vector.memset(sequence[:, 0:MARGIN], 0.0)
+        nc.vector.memset(sequence[:, MARGIN + TOKENS :], 0.0)
+        make_identity(nc, plus[:])
+        nc.scalar.mul(minus[:], plus[:], -1.0)
+
+        def look_up(place, first):
+            product = products.tile([FEATURES, PIECE], F32, name=f"product{place}")
+            shifted = MARGIN + first + place - MIDDLE
+            nc.vector.tensor_tensor(
+                product[:],
+                units[place][:].indirect(offsets[:, first // PER_COLUMN : (first + PIECE) // PER_COLUMN]),
+                sequence[:, shifted : shifted + PIECE],
+                MULT,
+            )
+            return product
+
+        def larger_of(a, b, ring, width=PIECE):
+            difference = differences.tile([FEATURES, PIECE], F32, name="difference")
+            nc.tensor.matmul(difference[:, :width], plus[:], a[:, :width], start=True, stop=False)
+            nc.tensor.matmul(difference[:, :width], minus[:], b[:, :width], start=False, stop=True)
+            larger = pairs.tile([FEATURES, PIECE], F32, name=f"pair{ring}")
+            nc.tensor.matmul(larger[:, :width], plus[:], b[:, :width], start=True, stop=False)
+            excess = products.tile([FEATURES, PIECE], F32, name="excess")
+            nc.scalar.activation(excess[:, :width], difference[:, :width], RELU)
+            nc.tensor.matmul(larger[:, :width], plus[:], excess[:, :width], start=False, stop=True)
+            return larger
+
+        def widen(running, other, name):
+            widened = maxima.tile([FEATURES, PIECE], F32, name=name)
+            nc.vector.tensor_tensor(widened[:], running[:], other[:], MAX)
+            return widened
+
+        def store(region, first, finished):
+            row = region * FEATURES
+            nc.sync.dma_start(out[row : row + FEATURES, first : first + PIECE], finished[:])
+
+        ring_maxima = {}
+        for ring in OUTER_RINGS:
+            for first in pieces:
+                a = look_up(ring, first)
+                b = look_up(PLACES - 1 - ring, first)
+                if (ring, first) == (OUTER_RINGS[-1], pieces[-1]):
+                    ring_maxima[(ring, first)] = larger_of(a, b, ring, width=SHARE)
+                    rest = maxima.tile([FEATURES, PIECE], F32, name="rest")
+                    nc.vector.tensor_tensor(rest[:, SHARE:], a[:, SHARE:], b[:, SHARE:], MAX)
+                else:
+                    ring_maxima[(ring, first)] = larger_of(a, b, ring)
+
+        running = {first: look_up(inner[0], first) for first in pieces}
+        for place in inner[1:]:
+            fresh = {first: look_up(place, first) for first in pieces}
+            for first in pieces:
+                running[first] = widen(running[first], fresh[first], f"upto{place}")
+        for first in pieces:
+            store(MIDDLE - 1, first, running[first])
+
+        for ring in OUTER_RINGS:
+            for first in pieces:
+                if (ring, first) == (OUTER_RINGS[-1], pieces[-1]):
+                    widened = maxima.tile([FEATURES, PIECE], F32, name=f"region{ring}")
+                    nc.vector.tensor_tensor(widened[:, SHARE:], running[first][:, SHARE:], rest[:, SHARE:], MAX)
+                    nc.vector.tensor_tensor(
+                        widened[:, :SHARE], running[first][:, :SHARE], ring_maxima[(ring, first)][:, :SHARE], MAX
+                    )
+                    running[first] = widened
+                else:
+                    running[first] = widen(running[first], ring_maxima[(ring, first)], f"region{ring}")
+                store(ring, first, running[first])

@@ -10,7 +10,7 @@ PIECE = 512
 PER_COLUMN = 16
 MARGIN = 8
 SHARE = 384
-OUTER_RINGS = (1, 0)
+ORDER = (2, 4, 1, 5, 3, 0, 6)
 
 F32 = mybir.dt.float32
 U16 = mybir.dt.uint16
@@ -22,18 +22,16 @@ RELU = mybir.ActivationFunctionType.Relu
 def tile_multiregionembeddinglayer_kernel(tc, u, seq_emb, offs, out):
     nc = tc.nc
     pieces = range(0, TOKENS, PIECE)
-    inner = [MIDDLE - 1, MIDDLE, MIDDLE + 1]
-    outer = [place for ring in OUTER_RINGS for place in (ring, PLACES - 1 - ring)]
     with (
         tc.tile_pool(name="held", bufs=1) as held,
         tc.tile_pool(name="products", bufs=2) as products,
         tc.tile_pool(name="maxima", bufs=2) as maxima,
         tc.psum_pool(name="differences", bufs=2) as differences,
-        tc.psum_pool(name="pairs", bufs=2) as pairs,
+        tc.psum_pool(name="pairs", bufs=1) as pairs,
     ):
         offsets = held.tile([FEATURES, TOKENS // PER_COLUMN], U16, name="offsets")
         sequence = held.tile([FEATURES, MARGIN + TOKENS + MARGIN], F32, name="sequence")
-        units = {place: held.tile([FEATURES, WORDS], F32, name=f"unit{place}") for place in outer + inner}
+        units = {place: held.tile([FEATURES, WORDS], F32, name=f"unit{place}") for place in ORDER}
         plus = held.tile([FEATURES, FEATURES], F32, name="plus")
         minus = held.tile([FEATURES, FEATURES], F32, name="minus")
 
@@ -44,8 +42,7 @@ def tile_multiregionembeddinglayer_kernel(tc, u, seq_emb, offs, out):
             return units[place][:], u[place * FEATURES : (place + 1) * FEATURES, :]
 
         nc.sync.dma_start(offsets[:], offs)
-        loads = [tokens(0, PIECE + MARGIN), unit(outer[0]), unit(outer[1]), tokens(PIECE + MARGIN, TOKENS)]
-        loads += [unit(place) for place in outer[2:] + inner]
+        loads = [tokens(0, PIECE + MARGIN)] + [unit(place) for place in ORDER] + [tokens(PIECE + MARGIN, TOKENS)]
         for turn, (tile_side, dram_side) in enumerate(loads):
             queue = nc.scalar if turn % 2 == 0 else nc.sync
             queue.dma_start(tile_side, dram_side)
@@ -65,55 +62,53 @@ def tile_multiregionembeddinglayer_kernel(tc, u, seq_emb, offs, out):
             )
             return product
 
-        def larger_of(a, b, ring, width=PIECE):
+        def larger_of(a, b, name, width=PIECE):
             difference = differences.tile([FEATURES, PIECE], F32, name="difference")
             nc.tensor.matmul(difference[:, :width], plus[:], a[:, :width], start=True, stop=False)
             nc.tensor.matmul(difference[:, :width], minus[:], b[:, :width], start=False, stop=True)
-            larger = pairs.tile([FEATURES, PIECE], F32, name=f"pair{ring}")
+            larger = pairs.tile([FEATURES, PIECE], F32, name=name)
             nc.tensor.matmul(larger[:, :width], plus[:], b[:, :width], start=True, stop=False)
             excess = products.tile([FEATURES, PIECE], F32, name="excess")
             nc.scalar.activation(excess[:, :width], difference[:, :width], RELU)
             nc.tensor.matmul(larger[:, :width], plus[:], excess[:, :width], start=False, stop=True)
             return larger
 
-        def widen(running, other, name):
-            widened = maxima.tile([FEATURES, PIECE], F32, name=name)
-            nc.vector.tensor_tensor(widened[:], running[:], other[:], MAX)
-            return widened
+        def maximum(a, b, name, columns=slice(0, PIECE), larger=None):
+            if larger is None:
+                larger = maxima.tile([FEATURES, PIECE], F32, name=name)
+            nc.vector.tensor_tensor(larger[:, columns], a[:, columns], b[:, columns], MAX)
+            return larger
 
-        def store(region, first, finished):
-            row = region * FEATURES
+        def store(number, first, finished):
+            row = number * FEATURES
             nc.sync.dma_start(out[row : row + FEATURES, first : first + PIECE], finished[:])
 
-        ring_maxima = {}
-        for ring in OUTER_RINGS:
-            for first in pieces:
-                a = look_up(ring, first)
-                b = look_up(PLACES - 1 - ring, first)
-                if (ring, first) == (OUTER_RINGS[-1], pieces[-1]):
-                    ring_maxima[(ring, first)] = larger_of(a, b, ring, width=SHARE)
-                    rest = maxima.tile([FEATURES, PIECE], F32, name="rest")
-                    nc.vector.tensor_tensor(rest[:, SHARE:], a[:, SHARE:], b[:, SHARE:], MAX)
-                else:
-                    ring_maxima[(ring, first)] = larger_of(a, b, ring)
+        def region(number, first, a, b):
+            finished = maximum(a, b, f"region{number}")
+            store(number, first, finished)
+            return finished
 
-        running = {first: look_up(inner[0], first) for first in pieces}
-        for place in inner[1:]:
-            fresh = {first: look_up(place, first) for first in pieces}
-            for first in pieces:
-                running[first] = widen(running[first], fresh[first], f"upto{place}")
-        for first in pieces:
-            store(MIDDLE - 1, first, running[first])
-
-        for ring in OUTER_RINGS:
-            for first in pieces:
-                if (ring, first) == (OUTER_RINGS[-1], pieces[-1]):
-                    widened = maxima.tile([FEATURES, PIECE], F32, name=f"region{ring}")
-                    nc.vector.tensor_tensor(widened[:, SHARE:], running[first][:, SHARE:], rest[:, SHARE:], MAX)
-                    nc.vector.tensor_tensor(
-                        widened[:, :SHARE], running[first][:, :SHARE], ring_maxima[(ring, first)][:, :SHARE], MAX
-                    )
-                    running[first] = widened
-                else:
-                    running[first] = widen(running[first], ring_maxima[(ring, first)], f"region{ring}")
-                store(ring, first, running[first])
+        early, late = pieces
+        early_24 = larger_of(look_up(2, early), look_up(4, early), "early_24")
+        early_15 = larger_of(look_up(1, early), look_up(5, early), "early_15")
+        early_3 = look_up(3, early)
+        early_06 = larger_of(look_up(0, early), look_up(6, early), "early_06")
+        early_region_of_3 = region(2, early, early_3, early_24)
+        late_0, late_6 = look_up(0, late), look_up(6, late)
+        late_06 = larger_of(late_0, late_6, "late_06", width=SHARE)
+        late_2 = look_up(2, late)
+        rest = slice(SHARE, PIECE)
+        late_06_rest = maximum(late_0, late_6, "late_06_rest", columns=rest)
+        early_region_of_5 = region(1, early, early_region_of_3, early_15)
+        late_4 = look_up(4, late)
+        late_3 = look_up(3, late)
+        late_24 = maximum(late_2, late_4, "late_24")
+        late_1 = look_up(1, late)
+        late_region_of_3 = region(2, late, late_24, late_3)
+        late_5 = look_up(5, late)
+        late_1_to_4 = maximum(late_region_of_3, late_1, "late_1_to_4")
+        late_region_of_5 = region(1, late, late_1_to_4, late_5)
+        region(0, early, early_region_of_5, early_06)
+        finished = maximum(late_region_of_5, late_06_rest, "region0", columns=rest)
+        maximum(late_region_of_5, late_06, "region0", columns=slice(0, SHARE), larger=finished)
+        store(0, late, finished)

@@ -7,10 +7,10 @@ MIDDLE = PLACES // 2
 WORDS = 512
 TOKENS = 1024
 PIECE = 512
+FIRST = 128
 PER_COLUMN = 16
 MARGIN = 8
-SHARE = 384
-ORDER = (2, 4, 1, 5, 3, 0, 6)
+ORDER = (2, 4, 3, 1, 5, 0, 6)
 
 F32 = mybir.dt.float32
 U16 = mybir.dt.uint16
@@ -27,7 +27,7 @@ def tile_multiregionembeddinglayer_kernel(tc, u, seq_emb, offs, out):
         tc.tile_pool(name="products", bufs=2) as products,
         tc.tile_pool(name="maxima", bufs=2) as maxima,
         tc.psum_pool(name="differences", bufs=2) as differences,
-        tc.psum_pool(name="pairs", bufs=1) as pairs,
+        tc.psum_pool(name="sums", bufs=1) as sums,
     ):
         offsets = held.tile([FEATURES, TOKENS // PER_COLUMN], U16, name="offsets")
         sequence = held.tile([FEATURES, MARGIN + TOKENS + MARGIN], F32, name="sequence")
@@ -42,46 +42,68 @@ def tile_multiregionembeddinglayer_kernel(tc, u, seq_emb, offs, out):
             return units[place][:], u[place * FEATURES : (place + 1) * FEATURES, :]
 
         nc.sync.dma_start(offsets[:], offs)
-        loads = [tokens(0, PIECE + MARGIN)] + [unit(place) for place in ORDER] + [tokens(PIECE + MARGIN, TOKENS)]
-        for turn, (tile_side, dram_side) in enumerate(loads):
-            queue = nc.scalar if turn % 2 == 0 else nc.sync
-            queue.dma_start(tile_side, dram_side)
+        loads = [unit(ORDER[0]), tokens(0, FIRST + MARGIN), tokens(FIRST + MARGIN, PIECE + MARGIN)]
+        loads += [unit(place) for place in ORDER[1:]]
+        loads += [tokens(PIECE + MARGIN, TOKENS)]
+        for tile_side, dram_side in loads:
+            nc.sync.dma_start(tile_side, dram_side)
         nc.vector.memset(sequence[:, 0:MARGIN], 0.0)
         nc.vector.memset(sequence[:, MARGIN + TOKENS :], 0.0)
         make_identity(nc, plus[:])
         nc.scalar.mul(minus[:], plus[:], -1.0)
 
-        def look_up(place, first):
-            product = products.tile([FEATURES, PIECE], F32, name=f"product{place}")
-            shifted = MARGIN + first + place - MIDDLE
-            nc.vector.tensor_tensor(
-                product[:],
-                units[place][:].indirect(offsets[:, first // PER_COLUMN : (first + PIECE) // PER_COLUMN]),
-                sequence[:, shifted : shifted + PIECE],
-                MULT,
-            )
+        def look_up(place, first, parts=(slice(0, PIECE),), product=None):
+            if product is None:
+                product = products.tile([FEATURES, PIECE], F32, name=f"product{place}")
+            shift = MARGIN + place - MIDDLE
+            for part in parts:
+                start, stop = first + part.start, first + part.stop
+                nc.vector.tensor_tensor(
+                    product[:, part],
+                    units[place][:].indirect(offsets[:, start // PER_COLUMN : stop // PER_COLUMN]),
+                    sequence[:, shift + start : shift + stop],
+                    MULT,
+                )
             return product
 
-        def larger_of(a, b, name, width=PIECE):
-            difference = differences.tile([FEATURES, PIECE], F32, name="difference")
-            nc.tensor.matmul(difference[:, :width], plus[:], a[:, :width], start=True, stop=False)
-            nc.tensor.matmul(difference[:, :width], minus[:], b[:, :width], start=False, stop=True)
-            larger = pairs.tile([FEATURES, PIECE], F32, name=name)
-            nc.tensor.matmul(larger[:, :width], plus[:], b[:, :width], start=True, stop=False)
+        def add(bank, product, weights=plus, start=False, stop=False):
+            nc.tensor.matmul(bank[:], weights[:], product[:], start=start, stop=stop)
+
+        def positive_part(difference):
             excess = products.tile([FEATURES, PIECE], F32, name="excess")
-            nc.scalar.activation(excess[:, :width], difference[:, :width], RELU)
-            nc.tensor.matmul(larger[:, :width], plus[:], excess[:, :width], start=False, stop=True)
+            nc.scalar.activation(excess[:], difference[:], RELU)
+            return excess
+
+        def larger_of(a, b, name):
+            difference = differences.tile([FEATURES, PIECE], F32, name="difference")
+            add(difference, a, start=True)
+            add(difference, b, weights=minus, stop=True)
+            larger = sums.tile([FEATURES, PIECE], F32, name=name)
+            add(larger, b, start=True)
+            add(larger, positive_part(difference), stop=True)
             return larger
 
-        def maximum(a, b, name, columns=slice(0, PIECE), larger=None):
-            if larger is None:
-                larger = maxima.tile([FEATURES, PIECE], F32, name=name)
-            nc.vector.tensor_tensor(larger[:, columns], a[:, columns], b[:, columns], MAX)
+        def largest_of(a, b, c, name):
+            first_difference = differences.tile([FEATURES, PIECE], F32, name="difference")
+            add(first_difference, a, start=True)
+            add(first_difference, b, weights=minus, stop=True)
+            second_difference = differences.tile([FEATURES, PIECE], F32, name="difference")
+            add(second_difference, b, start=True)
+            add(second_difference, c, weights=minus)
+            add(second_difference, positive_part(first_difference), stop=True)
+            largest = sums.tile([FEATURES, PIECE], F32, name=name)
+            add(largest, c, start=True)
+            add(largest, positive_part(second_difference), stop=True)
+            return largest
+
+        def maximum(a, b, name):
+            larger = maxima.tile([FEATURES, PIECE], F32, name=name)
+            nc.vector.tensor_tensor(larger[:], a[:], b[:], MAX)
             return larger
 
         def store(number, first, finished):
             row = number * FEATURES
-            nc.sync.dma_start(out[row : row + FEATURES, first : first + PIECE], finished[:])
+            nc.sync.dma_start(out[row : row + FEATURES, first : first + finished.shape[1]], finished[:])
 
         def region(number, first, a, b):
             finished = maximum(a, b, f"region{number}")
@@ -89,26 +111,28 @@ def tile_multiregionembeddinglayer_kernel(tc, u, seq_emb, offs, out):
             return finished
 
         early, late = pieces
-        early_24 = larger_of(look_up(2, early), look_up(4, early), "early_24")
+        early_2 = look_up(2, early, parts=(slice(0, FIRST), slice(FIRST, PIECE)))
+        early_4, early_3 = look_up(4, early), look_up(3, early)
+        inner = largest_of(early_2, early_4, early_3, "early_234")
+        region_of_3 = held.tile([FEATURES, TOKENS], F32, name="region_of_3")
+        early_region_of_3, late_region_of_3 = region_of_3[:, :PIECE], region_of_3[:, PIECE:]
+        nc.scalar.copy(early_region_of_3, inner[:])
         early_15 = larger_of(look_up(1, early), look_up(5, early), "early_15")
-        early_3 = look_up(3, early)
-        early_06 = larger_of(look_up(0, early), look_up(6, early), "early_06")
-        early_region_of_3 = region(2, early, early_3, early_24)
-        late_0, late_6 = look_up(0, late), look_up(6, late)
-        late_06 = larger_of(late_0, late_6, "late_06", width=SHARE)
-        late_2 = look_up(2, late)
-        rest = slice(SHARE, PIECE)
-        late_06_rest = maximum(late_0, late_6, "late_06_rest", columns=rest)
-        early_region_of_5 = region(1, early, early_region_of_3, early_15)
-        late_4 = look_up(4, late)
+        late_06 = larger_of(look_up(0, late), look_up(6, late), "late_06")
+        sides = [held.tile([FEATURES, 2 * PIECE], F32, name=name) for name in ("left", "right")]
+        for side, early_place, late_place in zip(sides, (0, 6), (2, 4)):
+            look_up(early_place, early, product=side[:, :PIECE])
+            look_up(late_place, late, product=side[:, PIECE:])
         late_3 = look_up(3, late)
-        late_24 = maximum(late_2, late_4, "late_24")
+        both = held.tile([FEATURES, 2 * PIECE], F32, name="both")
+        nc.vector.tensor_tensor(both[:], sides[0][:], sides[1][:], MAX)
+        early_06, late_24 = both[:, :PIECE], both[:, PIECE:]
         late_1 = look_up(1, late)
-        late_region_of_3 = region(2, late, late_24, late_3)
+        nc.vector.tensor_tensor(late_region_of_3, late_24[:], late_3[:], MAX)
+        store(2, early, region_of_3)
         late_5 = look_up(5, late)
         late_1_to_4 = maximum(late_region_of_3, late_1, "late_1_to_4")
+        early_region_of_5 = region(1, early, early_region_of_3, early_15)
         late_region_of_5 = region(1, late, late_1_to_4, late_5)
         region(0, early, early_region_of_5, early_06)
-        finished = maximum(late_region_of_5, late_06_rest, "region0", columns=rest)
-        maximum(late_region_of_5, late_06, "region0", columns=slice(0, SHARE), larger=finished)
-        store(0, late, finished)
+        region(0, late, late_region_of_5, late_06)

import concourse.mybir as mybir
from concourse.masks import make_identity

FEATURES = 128
PLACES = 7
MIDDLE = PLACES // 2
WORDS = 512
TOKENS = 1024
PIECE = 512
FIRST = 128
PER_COLUMN = 16
MARGIN = 8
ORDER = (2, 4, 3, 1, 5, 0, 6)

F32 = mybir.dt.float32
U16 = mybir.dt.uint16
MULT = mybir.AluOpType.mult
MAX = mybir.AluOpType.max
RELU = mybir.ActivationFunctionType.Relu


def tile_multiregionembeddinglayer_kernel(tc, u, seq_emb, offs, out):
    nc = tc.nc
    pieces = range(0, TOKENS, PIECE)
    with (
        tc.tile_pool(name="held", bufs=1) as held,
        tc.tile_pool(name="products", bufs=2) as products,
        tc.tile_pool(name="maxima", bufs=2) as maxima,
        tc.psum_pool(name="differences", bufs=2) as differences,
        tc.psum_pool(name="sums", bufs=1) as sums,
    ):
        offsets = held.tile([FEATURES, TOKENS // PER_COLUMN], U16, name="offsets")
        sequence = held.tile([FEATURES, MARGIN + TOKENS + MARGIN], F32, name="sequence")
        units = {place: held.tile([FEATURES, WORDS], F32, name=f"unit{place}") for place in ORDER}
        plus = held.tile([FEATURES, FEATURES], F32, name="plus")
        minus = held.tile([FEATURES, FEATURES], F32, name="minus")

        def tokens(start, stop):
            return sequence[:, MARGIN + start : MARGIN + stop], seq_emb[:, start:stop]

        def unit(place):
            return units[place][:], u[place * FEATURES : (place + 1) * FEATURES, :]

        nc.sync.dma_start(offsets[:], offs)
        loads = [unit(ORDER[0]), tokens(0, FIRST + MARGIN), tokens(FIRST + MARGIN, PIECE + MARGIN)]
        loads += [unit(place) for place in ORDER[1:]]
        loads += [tokens(PIECE + MARGIN, TOKENS)]
        for tile_side, dram_side in loads:
            nc.sync.dma_start(tile_side, dram_side)
        nc.vector.memset(sequence[:, 0:MARGIN], 0.0)
        nc.vector.memset(sequence[:, MARGIN + TOKENS :], 0.0)
        make_identity(nc, plus[:])
        nc.scalar.mul(minus[:], plus[:], -1.0)

        def look_up(place, first, parts=(slice(0, PIECE),), product=None):
            if product is None:
                product = products.tile([FEATURES, PIECE], F32, name=f"product{place}")
            shift = MARGIN + place - MIDDLE
            for part in parts:
                start, stop = first + part.start, first + part.stop
                nc.vector.tensor_tensor(
                    product[:, part],
                    units[place][:].indirect(offsets[:, start // PER_COLUMN : stop // PER_COLUMN]),
                    sequence[:, shift + start : shift + stop],
                    MULT,
                )
            return product

        def add(bank, product, weights=plus, start=False, stop=False):
            nc.tensor.matmul(bank[:], weights[:], product[:], start=start, stop=stop)

        def positive_part(difference):
            excess = products.tile([FEATURES, PIECE], F32, name="excess")
            nc.scalar.activation(excess[:], difference[:], RELU)
            return excess

        def larger_of(a, b, name):
            difference = differences.tile([FEATURES, PIECE], F32, name="difference")
            add(difference, a, start=True)
            add(difference, b, weights=minus, stop=True)
            larger = sums.tile([FEATURES, PIECE], F32, name=name)
            add(larger, b, start=True)
            add(larger, positive_part(difference), stop=True)
            return larger

        def largest_of(a, b, c, name):
            first_difference = differences.tile([FEATURES, PIECE], F32, name="difference")
            add(first_difference, a, start=True)
            add(first_difference, b, weights=minus, stop=True)
            second_difference = differences.tile([FEATURES, PIECE], F32, name="difference")
            add(second_difference, b, start=True)
            add(second_difference, c, weights=minus)
            add(second_difference, positive_part(first_difference), stop=True)
            largest = sums.tile([FEATURES, PIECE], F32, name=name)
            add(largest, c, start=True)
            add(largest, positive_part(second_difference), stop=True)
            return largest

        def maximum(a, b, name):
            larger = maxima.tile([FEATURES, PIECE], F32, name=name)
            nc.vector.tensor_tensor(larger[:], a[:], b[:], MAX)
            return larger

        def store(number, first, finished):
            row = number * FEATURES
            nc.sync.dma_start(out[row : row + FEATURES, first : first + finished.shape[1]], finished[:])

        def region(number, first, a, b):
            finished = maximum(a, b, f"region{number}")
            store(number, first, finished)
            return finished

        early, late = pieces
        early_2 = look_up(2, early, parts=(slice(0, FIRST), slice(FIRST, PIECE)))
        early_4, early_3 = look_up(4, early), look_up(3, early)
        inner = largest_of(early_2, early_4, early_3, "early_234")
        region_of_3 = held.tile([FEATURES, TOKENS], F32, name="region_of_3")
        early_region_of_3, late_region_of_3 = region_of_3[:, :PIECE], region_of_3[:, PIECE:]
        nc.scalar.copy(early_region_of_3, inner[:])
        early_15 = larger_of(look_up(1, early), look_up(5, early), "early_15")
        late_06 = larger_of(look_up(0, late), look_up(6, late), "late_06")
        sides = [held.tile([FEATURES, 2 * PIECE], F32, name=name) for name in ("left", "right")]
        for side, early_place, late_place in zip(sides, (0, 6), (2, 4)):
            look_up(early_place, early, product=side[:, :PIECE])
            look_up(late_place, late, product=side[:, PIECE:])
        late_3 = look_up(3, late)
        both = held.tile([FEATURES, 2 * PIECE], F32, name="both")
        nc.vector.tensor_tensor(both[:], sides[0][:], sides[1][:], MAX)
        early_06, late_24 = both[:, :PIECE], both[:, PIECE:]
        late_1 = look_up(1, late)
        nc.vector.tensor_tensor(late_region_of_3, late_24[:], late_3[:], MAX)
        store(2, early, region_of_3)
        late_5 = look_up(5, late)
        late_1_to_4 = maximum(late_region_of_3, late_1, "late_1_to_4")
        early_region_of_5 = region(1, early, early_region_of_3, early_15)
        late_region_of_5 = region(1, late, late_1_to_4, late_5)
        region(0, early, early_region_of_5, early_06)
        region(0, late, late_region_of_5, late_06)
